import numpy as np
import ml_dtypes


def mxq(x, axis, fmt="e4m3"):
    dtype, down = {"e4m3": (ml_dtypes.float8_e4m3fn, 7), "e5m2": (ml_dtypes.float8_e5m2, 14)}[fmt]
    v = np.moveaxis(np.asarray(x, np.float32).astype(ml_dtypes.bfloat16).astype(np.float64), axis, -1)
    blocks = v.reshape(v.shape[:-1] + (-1, 32))
    amax = np.abs(blocks).max(-1, keepdims=True)
    byte = np.maximum(np.where(amax > 0, np.frexp(amax)[1] - 1 + 127, 0) - down, 1)
    scale = np.exp2(byte - 127.0)
    codes = (blocks / scale).astype(np.float32).astype(dtype).astype(np.float64)
    return np.moveaxis((codes * scale).reshape(v.shape), -1, axis)


WIDE = False


def mx_kscale(k):
    if not WIDE:
        return np.ones(k)
    levels = np.array([10, -10, 5, -5, 0])
    a = np.random.permutation(np.resize(levels, k // 512 * 4)).reshape(k // 512, 4)
    idx = np.arange(k)
    return np.exp2(a[idx // 512, idx % 128 // 32])


BF16 = ml_dtypes.bfloat16


def bf(x):
    return np.asarray(x, np.float32).astype(BF16)


def f64(x):
    return np.asarray(x).astype(np.float64)


N1, N2, D = 2048, 2048, 512

SQRT5 = np.sqrt(5.0)


def setup_inputs():
    s = mx_kscale(D)
    g = np.random.standard_normal((1, D))
    x1 = np.random.standard_normal((N1, 1)) * g + 0.6 * np.random.standard_normal((N1, D))
    x2 = np.random.standard_normal((N2, 1)) * g + 0.6 * np.random.standard_normal((N2, D))
    x2[: N2 // 4] = x1[: N2 // 4]
    x1[-(N1 // 4):] *= (s * s)[None, :]
    x2[-(N2 // 4):] *= (s * s)[None, :]
    return {"X1": bf(x1), "X2": bf(x2),
            "c": bf(np.random.uniform(size=(1,)) + 0.5),
            "l": bf((np.random.uniform(size=(D,)) + 0.5) * 2.0 * np.sqrt(D))}


def reference(X1, X2, c, l):
    X1_l = f64(X1) / f64(l)
    X2_l = f64(X2) / f64(l)
    sq1 = np.sum(X1_l * X1_l, axis=-1)
    sq2 = np.sum(X2_l * X2_l, axis=-1)
    cross = mxq(X1_l, 1, "e4m3") @ mxq(X2_l, 1, "e4m3").T
    d2 = np.maximum(sq1[:, None] + sq2[None, :] - 2.0 * cross, 0.0)
    r = np.sqrt(d2)
    c2 = np.squeeze(f64(c) * f64(c))
    return c2 * (1.0 + SQRT5 * r + (5.0 / 3.0) * (r * r)) * np.exp(-SQRT5 * r)

@@ -1,0 +1,203 @@
+import math
+from contextlib import ExitStack
+
+from concourse import mybir
+from concourse.masks import make_identity
+
+F32 = mybir.dt.float32
+BF16 = mybir.dt.bfloat16
+U32 = mybir.dt.uint32
+U8 = mybir.dt.uint8
+FP8X4 = mybir.dt.float8_e4m3fn_x4
+ALU = mybir.AluOpType
+ACT = mybir.ActivationFunctionType
+
+P = 128
+PACK = 4
+D = P * PACK
+N_POINTS = 2048
+BLOCK = P
+GROUP = 4
+GROUP_POINTS = GROUP * BLOCK
+N_GROUPS = N_POINTS // GROUP_POINTS
+N_TILES = N_POINTS // BLOCK
+
+FLOPS = 2 * N_POINTS * N_POINTS * D
+
+
+def tile_matern52_kernel(tc, X1, X2, c, l, out):
+    nc = tc.nc
+    with ExitStack() as ctx:
+        keep = ctx.enter_context(tc.tile_pool(name="keep", bufs=1))
+        stage = ctx.enter_context(tc.tile_pool(name="stage", bufs=3))
+        dist_pool = ctx.enter_context(tc.tile_pool(name="dist", bufs=2 * GROUP))
+        poly_pool = ctx.enter_context(tc.tile_pool(name="poly", bufs=GROUP + 2))
+        psum_t = ctx.enter_context(tc.psum_pool(name="psum_t", bufs=3))
+        psum_b = ctx.enter_context(tc.psum_pool(name="psum_b", bufs=1))
+        psum_c = ctx.enter_context(tc.psum_pool(name="psum_c", bufs=4))
+        ctx.enter_context(tc.manual_schedule())
+
+        l_all = keep.tile([P, D], BF16)
+        nc.sync.dma_start(out=l_all[:], in_=l.partition_broadcast(P))
+        c_all = keep.tile([P, 1], BF16)
+        nc.scalar.dma_start(out=c_all[:], in_=c.partition_broadcast(P))
+        raw = {}
+        for name, points in (("x2", X2), ("x1", X1)):
+            for g in range(N_GROUPS):
+                rows = points[g * GROUP_POINTS : (g + 1) * GROUP_POINTS, :]
+                raw[name, g] = keep.tile([P, GROUP, D], BF16, name="raw_%s_%d" % (name, g))
+                nc.sync.dma_start(
+                    out=raw[name, g][:], in_=rows.rearrange("(b p) d -> p b d", p=P)
+                )
+
+        ident = keep.tile([P, P], F32)
+        make_identity(nc, ident[:])
+        one = keep.tile([P, 1], F32)
+        nc.vector.memset(one[:], 1.0)
+        warm = keep.tile([P, 1], F32)
+        nc.scalar.activation(out=warm[:], in_=one[:], func=ACT.Sqrt)
+        inv_l = keep.tile([P, D], F32)
+        nc.vector.reciprocal(out=inv_l[:], in_=l_all[:])
+        c_f32 = keep.tile([P, 1], F32)
+        nc.vector.tensor_copy(out=c_f32[:], in_=c_all[:])
+        poly_scale = keep.tile([P, 1], F32)
+        nc.vector.tensor_scalar(
+            out=poly_scale[:], in0=c_f32[:], scalar1=1.0 / math.sqrt(3.0), scalar2=None, op0=ALU.mult
+        )
+        poly_bias = keep.tile([P, 1], F32)
+        nc.vector.tensor_scalar(
+            out=poly_bias[:], in0=c_f32[:], scalar1=1.5 / math.sqrt(3.0), scalar2=None, op0=ALU.mult
+        )
+        poly_rest = keep.tile([P, 1], F32)
+        nc.vector.tensor_scalar(
+            out=poly_rest[:], in0=c_f32[:], scalar1=c_f32[:, 0:1], scalar2=0.25,
+            op0=ALU.mult, op1=ALU.mult,
+        )
+
+        codes = {}
+        scales = {}
+        squares = {}
+        for name in ("x1", "x2"):
+            codes[name] = keep.tile([P, N_POINTS], U32, name="codes_" + name, align_bytes=64)
+            scales[name] = keep.tile([P, N_POINTS], U8, name="scales_" + name, align_bytes=64)
+            squares[name] = keep.tile([P, N_TILES], F32, name="squares_" + name)
+        sq2_rows = keep.tile([P, N_POINTS], F32)
+
+        scaled = {}
+        grouped = {}
+
+        def scale(name, g):
+            scaled[name, g] = stage.tile([P, GROUP, D], F32, name="scaled")
+            nc.vector.tensor_tensor(
+                out=scaled[name, g][:],
+                in0=raw[name, g][:],
+                in1=inv_l[:].unsqueeze(1).to_broadcast([P, GROUP, D]),
+                op=ALU.mult,
+            )
+
+        def flip(name, g):
+            grouped[name, g] = stage.tile([P, GROUP_POINTS, PACK], BF16, name="grouped", align_bytes=64)
+            for b in range(GROUP):
+                block = scaled[name, g][:, b, :]
+                flipped = psum_t.tile([P, PACK, BLOCK], F32)
+                for t in range(PACK):
+                    nc.tensor.transpose(flipped[:, t, :], block[:, t * P : (t + 1) * P], ident[:])
+                target = grouped[name, g][:, b * BLOCK : (b + 1) * BLOCK, :]
+                source = flipped[:].rearrange("p t r -> p r t")
+                if b % 2 == 0:
+                    nc.scalar.copy(out=target, in_=source)
+                else:
+                    nc.vector.tensor_copy(out=target, in_=source)
+                unread = stage.tile([P, D], BF16)
+                nc.scalar.activation(
+                    out=unread[:], in_=block, func=ACT.Square,
+                    accum_out=squares[name][:, g * GROUP + b : g * GROUP + b + 1],
+                )
+
+        def quantise(name, g):
+            cols = slice(g * GROUP_POINTS, (g + 1) * GROUP_POINTS)
+            nc.vector.quantize_mx(
+                out=codes[name][:, cols].bitcast(FP8X4),
+                scales=scales[name][:, cols],
+                in_=grouped[name, g][:].rearrange("p r t -> p (r t)"),
+            )
+
+        def spread_sq2(g):
+            spread = psum_b.tile([P, GROUP_POINTS], F32)
+            for b in range(GROUP):
+                column = squares["x2"][:, g * GROUP + b : g * GROUP + b + 1]
+                nc.tensor.transpose(
+                    spread[:, b * BLOCK : (b + 1) * BLOCK], column.to_broadcast([P, P]), ident[:]
+                )
+            nc.scalar.copy(out=sq2_rows[:, g * GROUP_POINTS : (g + 1) * GROUP_POINTS], in_=spread[:])
+
+        dist = {}
+        poly = {}
+
+        def distances(i):
+            dist[i] = dist_pool.tile([P, N_POINTS], F32, name="dist")
+            for j in range(N_GROUPS):
+                cols = slice(j * GROUP_POINTS, (j + 1) * GROUP_POINTS)
+                cross = psum_c.tile([P, GROUP_POINTS], F32)
+                nc.tensor.matmul_mx(
+                    out=cross[:],
+                    lhsT=codes["x1"][:, i * BLOCK : (i + 1) * BLOCK].bitcast(FP8X4),
+                    lhsT_scale=scales["x1"][:, i * BLOCK : (i + 1) * BLOCK],
+                    rhs=codes["x2"][:, cols].bitcast(FP8X4),
+                    rhs_scale=scales["x2"][:, cols],
+                    start=True, stop=True,
+                )
+                nc.vector.scalar_tensor_tensor(
+                    out=dist[i][:, cols], in0=cross[:], scalar=-2.0, in1=sq2_rows[:, cols],
+                    op0=ALU.mult, op1=ALU.add,
+                )
+            nc.vector.tensor_scalar(
+                out=dist[i][:], in0=dist[i][:], scalar1=squares["x1"][:, i : i + 1], scalar2=0.0,
+                op0=ALU.add, op1=ALU.max,
+            )
+
+        def root_and_polynomial(i):
+            nc.scalar.activation(out=dist[i][:], in_=dist[i][:], func=ACT.Sqrt, scale=5.0)
+            poly[i] = poly_pool.tile([P, N_POINTS], F32, name="poly")
+            nc.scalar.activation(
+                out=poly[i][:], in_=dist[i][:], func=ACT.Square,
+                scale=poly_scale[:, 0:1], bias=poly_bias[:, 0:1],
+            )
+
+        def finish(i):
+            nc.scalar.activation(out=dist[i][:], in_=dist[i][:], func=ACT.Exp, scale=-1.0)
+            nc.vector.scalar_tensor_tensor(
+                out=poly[i][:], in0=poly[i][:], scalar=poly_rest[:, 0:1], in1=dist[i][:],
+                op0=ALU.add, op1=ALU.mult,
+            )
+            nc.sync.dma_start(out=out[i * BLOCK : (i + 1) * BLOCK, :], in_=poly[i][:])
+
+        def batch(b):
+            return range(b * GROUP, (b + 1) * GROUP)
+
+        first = [("x2", g) for g in range(N_GROUPS)] + [("x1", 0), ("x1", 1)]
+        scale(*first[0])
+        for k in range(len(first)):
+            if k + 1 < len(first):
+                scale(*first[k + 1])
+            flip(*first[k])
+            if k >= 1:
+                quantise(*first[k - 1])
+                if first[k - 1][0] == "x2":
+                    spread_sq2(first[k - 1][1])
+        quantise(*first[-1])
+        for i in batch(0):
+            distances(i)
+
+        for b in range(N_GROUPS):
+            for i in batch(b):
+                root_and_polynomial(i)
+            if b + 1 < N_GROUPS:
+                for i in batch(b + 1):
+                    distances(i)
+            if b + 2 < N_GROUPS:
+                scale("x1", b + 2)
+                flip("x1", b + 2)
+                quantise("x1", b + 2)
+            for i in batch(b):
+                finish(i)

@@ -17,10 +17,18 @@ PACK = 4
 D = P * PACK
 N_POINTS = 2048
 BLOCK = P
-GROUP = 4
-GROUP_POINTS = GROUP * BLOCK
-N_GROUPS = N_POINTS // GROUP_POINTS
+BANK_POINTS = 2 * BLOCK
+GROUP_POINTS = 4 * BLOCK
+LOAD_POINTS = 8 * BLOCK
 N_TILES = N_POINTS // BLOCK
+N_BANKS = N_POINTS // BANK_POINTS
+N_GROUPS = N_POINTS // GROUP_POINTS
+N_LOADS = N_POINTS // LOAD_POINTS
+
+SLOTS = 25
+EARLY = (0, 2, 4, 6, 8, 10)
+HORNER = (12, 13, 14, 15)
+HORNER_AT = {0: (12, 13), 4: (14,), 8: (15,)}
 
 FLOPS = 2 * N_POINTS * N_POINTS * D
 
@@ -29,26 +37,26 @@ def tile_matern52_kernel(tc, X1, X2, c, l, out):
     nc = tc.nc
     with ExitStack() as ctx:
         keep = ctx.enter_context(tc.tile_pool(name="keep", bufs=1))
-        stage = ctx.enter_context(tc.tile_pool(name="stage", bufs=3))
-        dist_pool = ctx.enter_context(tc.tile_pool(name="dist", bufs=2 * GROUP))
-        poly_pool = ctx.enter_context(tc.tile_pool(name="poly", bufs=GROUP + 2))
+        big = ctx.enter_context(tc.tile_pool(name="big", bufs=SLOTS))
         psum_t = ctx.enter_context(tc.psum_pool(name="psum_t", bufs=3))
-        psum_b = ctx.enter_context(tc.psum_pool(name="psum_b", bufs=1))
-        psum_c = ctx.enter_context(tc.psum_pool(name="psum_c", bufs=4))
+        psum_s = ctx.enter_context(tc.psum_pool(name="psum_s", bufs=1))
+        psum_c = ctx.enter_context(tc.psum_pool(name="psum_c", bufs=3))
         ctx.enter_context(tc.manual_schedule())
 
-        l_all = keep.tile([P, D], BF16)
-        nc.sync.dma_start(out=l_all[:], in_=l.partition_broadcast(P))
+        l_cols = keep.tile([P, PACK], BF16)
+        nc.sync.dma_start(out=l_cols[:], in_=l.rearrange("(p t) -> p t", t=PACK))
         c_all = keep.tile([P, 1], BF16)
         nc.scalar.dma_start(out=c_all[:], in_=c.partition_broadcast(P))
         raw = {}
-        for name, points in (("x2", X2), ("x1", X1)):
-            for g in range(N_GROUPS):
-                rows = points[g * GROUP_POINTS : (g + 1) * GROUP_POINTS, :]
-                raw[name, g] = keep.tile([P, GROUP, D], BF16, name="raw_%s_%d" % (name, g))
-                nc.sync.dma_start(
-                    out=raw[name, g][:], in_=rows.rearrange("(b p) d -> p b d", p=P)
-                )
+        for h in range(N_LOADS):
+            for name, points in (("x2", X2), ("x1", X1)):
+                raw[name, h] = big.tile([P, LOAD_POINTS // BLOCK, D], BF16, name="raw", tag="big", align_bytes=64)
+                for q in range(2):
+                    first = h * LOAD_POINTS + q * GROUP_POINTS
+                    nc.sync.dma_start(
+                        out=raw[name, h][:, 4 * q : 4 * q + 4, :],
+                        in_=points[first : first + GROUP_POINTS, :].rearrange("(b p) d -> p b d", p=P),
+                    )
 
         ident = keep.tile([P, P], F32)
         make_identity(nc, ident[:])
@@ -56,8 +64,10 @@ def tile_matern52_kernel(tc, X1, X2, c, l, out):
         nc.vector.memset(one[:], 1.0)
         warm = keep.tile([P, 1], F32)
         nc.scalar.activation(out=warm[:], in_=one[:], func=ACT.Sqrt)
-        inv_l = keep.tile([P, D], F32)
-        nc.vector.reciprocal(out=inv_l[:], in_=l_all[:])
+        inv_l = keep.tile([P, PACK], F32)
+        nc.vector.reciprocal(out=inv_l[:], in_=l_cols[:])
+        inv_l2 = keep.tile([P, PACK], F32)
+        nc.vector.tensor_tensor(out=inv_l2[:], in0=inv_l[:], in1=inv_l[:], op=ALU.mult)
         c_f32 = keep.tile([P, 1], F32)
         nc.vector.tensor_copy(out=c_f32[:], in_=c_all[:])
         poly_scale = keep.tile([P, 1], F32)
@@ -74,68 +84,98 @@ def tile_matern52_kernel(tc, X1, X2, c, l, out):
             op0=ALU.mult, op1=ALU.mult,
         )
 
+        c2 = keep.tile([P, 1], F32)
+        nc.vector.tensor_tensor(out=c2[:], in0=c_f32[:], in1=c_f32[:], op=ALU.mult)
+        c2_third = keep.tile([P, 1], F32)
+        nc.vector.tensor_scalar(
+            out=c2_third[:], in0=c_f32[:], scalar1=c_f32[:, 0:1], scalar2=1.0 / 3.0,
+            op0=ALU.mult, op1=ALU.mult,
+        )
+
         codes = {}
         scales = {}
-        squares = {}
         for name in ("x1", "x2"):
             codes[name] = keep.tile([P, N_POINTS], U32, name="codes_" + name, align_bytes=64)
             scales[name] = keep.tile([P, N_POINTS], U8, name="scales_" + name, align_bytes=64)
-            squares[name] = keep.tile([P, N_TILES], F32, name="squares_" + name)
+        sq1 = keep.tile([P, N_TILES], F32)
         sq2_rows = keep.tile([P, N_POINTS], F32)
 
-        scaled = {}
+        flipped = {}
         grouped = {}
+        squared = {}
 
-        def scale(name, g):
-            scaled[name, g] = stage.tile([P, GROUP, D], F32, name="scaled")
+        def flip(name, k):
+            h, b = divmod(2 * k, LOAD_POINTS // BLOCK)
+            words = raw[name, h][:].bitcast(F32)
+            flipped[name, k] = psum_t.tile([P, 2, BANK_POINTS], F32, name="flipped")
+            for s in range(2):
+                for u in range(2):
+                    nc.tensor.transpose(
+                        flipped[name, k][:, u, s * BLOCK : (s + 1) * BLOCK],
+                        words[:, b + s, u : D // 2 : 2],
+                        ident[:],
+                    )
+
+        def divide(name, k):
+            g, half = divmod(k, 2)
+            if half == 0 and name == "x2":
+                both = big.tile([P, 2, GROUP_POINTS, PACK], BF16, name="grouped", tag="big", align_bytes=64)
+                grouped["x2", g] = both[:, 0, :, :]
+                grouped["x1", g] = both[:, 1, :, :]
             nc.vector.tensor_tensor(
-                out=scaled[name, g][:],
-                in0=raw[name, g][:],
-                in1=inv_l[:].unsqueeze(1).to_broadcast([P, GROUP, D]),
+                out=grouped[name, g][:, half * BANK_POINTS : (half + 1) * BANK_POINTS, :].rearrange(
+                    "p r (u e) -> p r u e", e=2
+                ),
+                in0=flipped[name, k][:].bitcast(BF16).rearrange("p u (r e) -> p r u e", e=2),
+                in1=inv_l[:].rearrange("p (u e) -> p u e", e=2).unsqueeze(1).to_broadcast([P, BANK_POINTS, 2, 2]),
                 op=ALU.mult,
             )
 
-        def flip(name, g):
-            grouped[name, g] = stage.tile([P, GROUP_POINTS, PACK], BF16, name="grouped", align_bytes=64)
-            for b in range(GROUP):
-                block = scaled[name, g][:, b, :]
-                flipped = psum_t.tile([P, PACK, BLOCK], F32)
-                for t in range(PACK):
-                    nc.tensor.transpose(flipped[:, t, :], block[:, t * P : (t + 1) * P], ident[:])
-                target = grouped[name, g][:, b * BLOCK : (b + 1) * BLOCK, :]
-                source = flipped[:].rearrange("p t r -> p r t")
-                if b % 2 == 0:
-                    nc.scalar.copy(out=target, in_=source)
-                else:
-                    nc.vector.tensor_copy(out=target, in_=source)
-                unread = stage.tile([P, D], BF16)
-                nc.scalar.activation(
-                    out=unread[:], in_=block, func=ACT.Square,
-                    accum_out=squares[name][:, g * GROUP + b : g * GROUP + b + 1],
+        def square(name, k):
+            if k % 2 == 0:
+                squared[name, k // 2] = big.tile(
+                    [P, 2, PACK, BANK_POINTS], F32, name="squared", tag="big", align_bytes=64
                 )
+            target = squared[name, k // 2][:, k % 2, :, :]
+            nc.scalar.activation(
+                out=target.rearrange("p (u e) r -> p u e r", e=2),
+                in_=flipped[name, k][:].bitcast(BF16).rearrange("p u (r e) -> p u e r", e=2),
+                func=ACT.Square,
+            )
 
         def quantise(name, g):
             cols = slice(g * GROUP_POINTS, (g + 1) * GROUP_POINTS)
             nc.vector.quantize_mx(
                 out=codes[name][:, cols].bitcast(FP8X4),
                 scales=scales[name][:, cols],
-                in_=grouped[name, g][:].rearrange("p r t -> p (r t)"),
+                in_=grouped[name, g].rearrange("p r t -> p (r t)"),
             )
 
-        def spread_sq2(g):
-            spread = psum_b.tile([P, GROUP_POINTS], F32)
-            for b in range(GROUP):
-                column = squares["x2"][:, g * GROUP + b : g * GROUP + b + 1]
-                nc.tensor.transpose(
-                    spread[:, b * BLOCK : (b + 1) * BLOCK], column.to_broadcast([P, P]), ident[:]
+        def sum_rows(k):
+            total = psum_s.tile([P, BANK_POINTS], F32, name="total")
+            for t in range(PACK):
+                nc.tensor.matmul(
+                    out=total[:], lhsT=inv_l2[:, t : t + 1].to_broadcast([P, P]), rhs=squared["x2", k // 2][:, k % 2, t, :],
+                    start=(t == 0), stop=(t == PACK - 1),
                 )
-            nc.scalar.copy(out=sq2_rows[:, g * GROUP_POINTS : (g + 1) * GROUP_POINTS], in_=spread[:])
+            nc.scalar.copy(out=sq2_rows[:, k * BANK_POINTS : (k + 1) * BANK_POINTS], in_=total[:])
+
+        def sum_column(i):
+            column = psum_s.tile([P, 1], F32, name="column")
+            for t in range(PACK):
+                nc.tensor.matmul(
+                    out=column[:],
+                    lhsT=squared["x1", i // 4][:, (i // 2) % 2, t, (i % 2) * BLOCK : (i % 2 + 1) * BLOCK],
+                    rhs=inv_l2[:, t : t + 1],
+                    start=(t == 0), stop=(t == PACK - 1),
+                )
+            nc.scalar.copy(out=sq1[:, i : i + 1], in_=column[:])
 
         dist = {}
         poly = {}
 
         def distances(i):
-            dist[i] = dist_pool.tile([P, N_POINTS], F32, name="dist")
+            dist[i] = big.tile([P, N_POINTS], F32, name="dist", tag="big", align_bytes=64)
             for j in range(N_GROUPS):
                 cols = slice(j * GROUP_POINTS, (j + 1) * GROUP_POINTS)
                 cross = psum_c.tile([P, GROUP_POINTS], F32)
@@ -152,52 +192,67 @@ def tile_matern52_kernel(tc, X1, X2, c, l, out):
                     op0=ALU.mult, op1=ALU.add,
                 )
             nc.vector.tensor_scalar(
-                out=dist[i][:], in0=dist[i][:], scalar1=squares["x1"][:, i : i + 1], scalar2=0.0,
+                out=dist[i][:], in0=dist[i][:], scalar1=sq1[:, i : i + 1], scalar2=0.0,
                 op0=ALU.add, op1=ALU.max,
             )
 
-        def root_and_polynomial(i):
+        def root(i):
             nc.scalar.activation(out=dist[i][:], in_=dist[i][:], func=ACT.Sqrt, scale=5.0)
-            poly[i] = poly_pool.tile([P, N_POINTS], F32, name="poly")
+
+        def polynomial(i):
+            poly[i] = big.tile([P, N_POINTS], F32, name="poly", tag="big", align_bytes=64)
             nc.scalar.activation(
                 out=poly[i][:], in_=dist[i][:], func=ACT.Square,
                 scale=poly_scale[:, 0:1], bias=poly_bias[:, 0:1],
             )
 
+        def horner(i):
+            poly[i] = big.tile([P, N_POINTS], F32, name="poly", tag="big", align_bytes=64)
+            nc.vector.tensor_scalar(
+                out=poly[i][:], in0=dist[i][:], scalar1=c2_third[:, 0:1], scalar2=c2[:, 0:1],
+                op0=ALU.mult, op1=ALU.add,
+            )
+            nc.vector.tensor_tensor(out=poly[i][:], in0=poly[i][:], in1=dist[i][:], op=ALU.mult)
+
         def finish(i):
             nc.scalar.activation(out=dist[i][:], in_=dist[i][:], func=ACT.Exp, scale=-1.0)
+            rest = c2 if i in HORNER else poly_rest
             nc.vector.scalar_tensor_tensor(
-                out=poly[i][:], in0=poly[i][:], scalar=poly_rest[:, 0:1], in1=dist[i][:],
+                out=poly[i][:], in0=poly[i][:], scalar=rest[:, 0:1], in1=dist[i][:],
                 op0=ALU.add, op1=ALU.mult,
             )
             nc.sync.dma_start(out=out[i * BLOCK : (i + 1) * BLOCK, :], in_=poly[i][:])
 
-        def batch(b):
-            return range(b * GROUP, (b + 1) * GROUP)
-
-        first = [("x2", g) for g in range(N_GROUPS)] + [("x1", 0), ("x1", 1)]
-        scale(*first[0])
-        for k in range(len(first)):
-            if k + 1 < len(first):
-                scale(*first[k + 1])
-            flip(*first[k])
+        for k in range(N_BANKS):
+            flip("x2", k)
+            flip("x1", k)
+            divide("x2", k)
+            square("x2", k)
+            if k >= 2 and k % 2 == 0:
+                quantise("x2", k // 2 - 1)
+            divide("x1", k)
+            square("x1", k)
+            if k >= 2 and k % 2 == 0:
+                quantise("x1", k // 2 - 1)
             if k >= 1:
-                quantise(*first[k - 1])
-                if first[k - 1][0] == "x2":
-                    spread_sq2(first[k - 1][1])
-        quantise(*first[-1])
-        for i in batch(0):
-            distances(i)
+                sum_rows(k - 1)
+        sum_rows(N_BANKS - 1)
+        quantise("x2", N_GROUPS - 1)
+        quantise("x1", N_GROUPS - 1)
+        sum_column(0)
+        sum_column(1)
 
-        for b in range(N_GROUPS):
-            for i in batch(b):
-                root_and_polynomial(i)
-            if b + 1 < N_GROUPS:
-                for i in batch(b + 1):
-                    distances(i)
-            if b + 2 < N_GROUPS:
-                scale("x1", b + 2)
-                flip("x1", b + 2)
-                quantise("x1", b + 2)
-            for i in batch(b):
-                finish(i)
+        for i in range(N_TILES):
+            distances(i)
+            if i + 2 < N_TILES:
+                sum_column(i + 2)
+            root(i)
+            if i in EARLY:
+                polynomial(i)
+
+        for i in range(N_TILES):
+            for h in HORNER_AT.get(i, ()):
+                horner(h)
+            if i not in EARLY and i not in HORNER:
+                polynomial(i)
+            finish(i)

@@ -24,11 +24,10 @@ N_TILES = N_POINTS // BLOCK
 N_BANKS = N_POINTS // BANK_POINTS
 N_GROUPS = N_POINTS // GROUP_POINTS
 N_LOADS = N_POINTS // LOAD_POINTS
-
-SLOTS = 25
-EARLY = (0, 2, 4, 6, 8, 10)
-HORNER = (12, 13, 14, 15)
-HORNER_AT = {0: (12, 13), 4: (14,), 8: (15,)}
+QUAD = 4
+LAG = 2
+AHEAD = 4
+UNIT = 4 * N_POINTS
 
 FLOPS = 2 * N_POINTS * N_POINTS * D
 
@@ -37,11 +36,13 @@ def tile_matern52_kernel(tc, X1, X2, c, l, out):
     nc = tc.nc
     with ExitStack() as ctx:
         keep = ctx.enter_context(tc.tile_pool(name="keep", bufs=1))
-        big = ctx.enter_context(tc.tile_pool(name="big", bufs=SLOTS))
-        psum_t = ctx.enter_context(tc.psum_pool(name="psum_t", bufs=3))
+        big = ctx.enter_context(tc.tile_pool(name="big", bufs=1))
+        psum = ctx.enter_context(tc.psum_pool(name="psum", bufs=7))
         psum_s = ctx.enter_context(tc.psum_pool(name="psum_s", bufs=1))
-        psum_c = ctx.enter_context(tc.psum_pool(name="psum_c", bufs=3))
         ctx.enter_context(tc.manual_schedule())
+
+        def place(shape, dtype, name, units):
+            return big.tile(shape, dtype, name=name, offset=int(units * UNIT), align_bytes=64)
 
         l_cols = keep.tile([P, PACK], BF16)
         nc.sync.dma_start(out=l_cols[:], in_=l.rearrange("(p t) -> p t", t=PACK))
@@ -49,8 +50,8 @@ def tile_matern52_kernel(tc, X1, X2, c, l, out):
         nc.scalar.dma_start(out=c_all[:], in_=c.partition_broadcast(P))
         raw = {}
         for h in range(N_LOADS):
-            for name, points in (("x2", X2), ("x1", X1)):
-                raw[name, h] = big.tile([P, LOAD_POINTS // BLOCK, D], BF16, name="raw", tag="big", align_bytes=64)
+            for s, (name, points) in enumerate((("x2", X2), ("x1", X1))):
+                raw[name, h] = place([P, LOAD_POINTS // BLOCK, D], BF16, "raw_%s_%d" % (name, h), 8 + 2 * h + s)
                 for q in range(2):
                     first = h * LOAD_POINTS + q * GROUP_POINTS
                     nc.sync.dma_start(
@@ -83,7 +84,6 @@ def tile_matern52_kernel(tc, X1, X2, c, l, out):
             out=poly_rest[:], in0=c_f32[:], scalar1=c_f32[:, 0:1], scalar2=0.25,
             op0=ALU.mult, op1=ALU.mult,
         )
-
         c2 = keep.tile([P, 1], F32)
         nc.vector.tensor_tensor(out=c2[:], in0=c_f32[:], in1=c_f32[:], op=ALU.mult)
         c2_third = keep.tile([P, 1], F32)
@@ -92,22 +92,34 @@ def tile_matern52_kernel(tc, X1, X2, c, l, out):
             op0=ALU.mult, op1=ALU.mult,
         )
 
-        codes = {}
-        scales = {}
-        for name in ("x1", "x2"):
-            codes[name] = keep.tile([P, N_POINTS], U32, name="codes_" + name, align_bytes=64)
-            scales[name] = keep.tile([P, N_POINTS], U8, name="scales_" + name, align_bytes=64)
+        codes = {"x1": place([P, N_POINTS], U32, "codes_x1", 25), "x2": place([P, N_POINTS], U32, "codes_x2", 26)}
+        sq2_rows = place([P, N_POINTS], F32, "sq2_rows", 27)
+        scales = {"x1": place([P, N_POINTS], U8, "scales_x1", 28), "x2": place([P, N_POINTS], U8, "scales_x2", 28.25)}
         sq1 = keep.tile([P, N_TILES], F32)
-        sq2_rows = keep.tile([P, N_POINTS], F32)
 
+        turned = psum_s.tile([P, PACK, P], F32, name="total")
+        for t in range(PACK):
+            nc.tensor.transpose(turned[:, t, :], inv_l[:, t : t + 1].to_broadcast([P, P]), ident[:])
+        inv_l_row = keep.tile([P, D], F32)
+        nc.scalar.copy(
+            out=inv_l_row[:].rearrange("p (j t) -> p j t", t=PACK), in_=turned[:].rearrange("p t j -> p j t")
+        )
+
+        scaled = {}
         flipped = {}
         grouped = {}
         squared = {}
+        for g in range(N_GROUPS):
+            both = place([P, 2, GROUP_POINTS, PACK], BF16, "grouped_%d" % g, 16 + g)
+            grouped["x2", g] = both[:, 0, :, :]
+            grouped["x1", g] = both[:, 1, :, :]
+            squared["x2", g] = place([P, PACK, GROUP_POINTS], F32, "squared_x2_%d" % g, 20 + g)
+            scaled[g] = place([P, QUAD, D], F32, "scaled_%d" % g, 12 + g)
 
         def flip(name, k):
             h, b = divmod(2 * k, LOAD_POINTS // BLOCK)
             words = raw[name, h][:].bitcast(F32)
-            flipped[name, k] = psum_t.tile([P, 2, BANK_POINTS], F32, name="flipped")
+            flipped[name, k] = psum.tile([P, 2, BANK_POINTS], F32, name="flipped", tag="bank")
             for s in range(2):
                 for u in range(2):
                     nc.tensor.transpose(
@@ -118,10 +130,6 @@ def tile_matern52_kernel(tc, X1, X2, c, l, out):
 
         def divide(name, k):
             g, half = divmod(k, 2)
-            if half == 0 and name == "x2":
-                both = big.tile([P, 2, GROUP_POINTS, PACK], BF16, name="grouped", tag="big", align_bytes=64)
-                grouped["x2", g] = both[:, 0, :, :]
-                grouped["x1", g] = both[:, 1, :, :]
             nc.vector.tensor_tensor(
                 out=grouped[name, g][:, half * BANK_POINTS : (half + 1) * BANK_POINTS, :].rearrange(
                     "p r (u e) -> p r u e", e=2
@@ -132,13 +140,11 @@ def tile_matern52_kernel(tc, X1, X2, c, l, out):
             )
 
         def square(name, k):
-            if k % 2 == 0:
-                squared[name, k // 2] = big.tile(
-                    [P, 2, PACK, BANK_POINTS], F32, name="squared", tag="big", align_bytes=64
-                )
-            target = squared[name, k // 2][:, k % 2, :, :]
+            g, half = divmod(k, 2)
             nc.scalar.activation(
-                out=target.rearrange("p (u e) r -> p u e r", e=2),
+                out=squared[name, g][:, :, half * BANK_POINTS : (half + 1) * BANK_POINTS].rearrange(
+                    "p (u e) r -> p u e r", e=2
+                ),
                 in_=flipped[name, k][:].bitcast(BF16).rearrange("p u (r e) -> p u e r", e=2),
                 func=ACT.Square,
             )
@@ -151,34 +157,43 @@ def tile_matern52_kernel(tc, X1, X2, c, l, out):
                 in_=grouped[name, g].rearrange("p r t -> p (r t)"),
             )
 
-        def sum_rows(k):
-            total = psum_s.tile([P, BANK_POINTS], F32, name="total")
-            for t in range(PACK):
-                nc.tensor.matmul(
-                    out=total[:], lhsT=inv_l2[:, t : t + 1].to_broadcast([P, P]), rhs=squared["x2", k // 2][:, k % 2, t, :],
-                    start=(t == 0), stop=(t == PACK - 1),
-                )
-            nc.scalar.copy(out=sq2_rows[:, k * BANK_POINTS : (k + 1) * BANK_POINTS], in_=total[:])
+        totals = {}
 
-        def sum_column(i):
-            column = psum_s.tile([P, 1], F32, name="column")
+        def sum_rows(g):
+            totals[g] = psum_s.tile([P, GROUP_POINTS], F32, name="total")
             for t in range(PACK):
                 nc.tensor.matmul(
-                    out=column[:],
-                    lhsT=squared["x1", i // 4][:, (i // 2) % 2, t, (i % 2) * BLOCK : (i % 2 + 1) * BLOCK],
-                    rhs=inv_l2[:, t : t + 1],
+                    out=totals[g][:], lhsT=inv_l2[:, t : t + 1].to_broadcast([P, P]), rhs=squared["x2", g][:, t, :],
                     start=(t == 0), stop=(t == PACK - 1),
                 )
-            nc.scalar.copy(out=sq1[:, i : i + 1], in_=column[:])
+
+        def keep_rows(g):
+            nc.vector.tensor_copy(out=sq2_rows[:, g * GROUP_POINTS : (g + 1) * GROUP_POINTS], in_=totals[g][:])
+
+        def divide_rows(g):
+            h, q = divmod(g, 2)
+            nc.gpsimd.tensor_tensor(
+                out=scaled[g][:], in0=raw["x1", h][:, QUAD * q : QUAD * (q + 1), :],
+                in1=inv_l_row[:].unsqueeze(1).to_broadcast([P, QUAD, D]), op=ALU.mult,
+            )
+
+        def sum_columns(g):
+            for b in range(QUAD):
+                nc.scalar.activation(
+                    out=scaled[g][:, b, :], in_=scaled[g][:, b, :], func=ACT.Square,
+                    accum_out=sq1[:, QUAD * g + b : QUAD * g + b + 1],
+                )
 
         dist = {}
         poly = {}
 
         def distances(i):
-            dist[i] = big.tile([P, N_POINTS], F32, name="dist", tag="big", align_bytes=64)
+            q, s = divmod(i, QUAD)
+            if s == 0:
+                dist[q] = place([P, QUAD, N_POINTS], F32, "dist_%d" % q, QUAD * q)
             for j in range(N_GROUPS):
                 cols = slice(j * GROUP_POINTS, (j + 1) * GROUP_POINTS)
-                cross = psum_c.tile([P, GROUP_POINTS], F32)
+                cross = psum.tile([P, GROUP_POINTS], F32, name="cross", tag="bank")
                 nc.tensor.matmul_mx(
                     out=cross[:],
                     lhsT=codes["x1"][:, i * BLOCK : (i + 1) * BLOCK].bitcast(FP8X4),
@@ -188,71 +203,99 @@ def tile_matern52_kernel(tc, X1, X2, c, l, out):
                     start=True, stop=True,
                 )
                 nc.vector.scalar_tensor_tensor(
-                    out=dist[i][:, cols], in0=cross[:], scalar=-2.0, in1=sq2_rows[:, cols],
+                    out=dist[q][:, s, cols], in0=cross[:], scalar=-2.0, in1=sq2_rows[:, cols],
                     op0=ALU.mult, op1=ALU.add,
                 )
             nc.vector.tensor_scalar(
-                out=dist[i][:], in0=dist[i][:], scalar1=sq1[:, i : i + 1], scalar2=0.0,
+                out=dist[q][:, s, :], in0=dist[q][:, s, :], scalar1=sq1[:, i : i + 1], scalar2=0.0,
                 op0=ALU.add, op1=ALU.max,
             )
 
-        def root(i):
-            nc.scalar.activation(out=dist[i][:], in_=dist[i][:], func=ACT.Sqrt, scale=5.0)
+        def tiles(first, count):
+            q, s = divmod(first, QUAD)
+            return dist[q][:, s : s + count, :]
 
-        def polynomial(i):
-            poly[i] = big.tile([P, N_POINTS], F32, name="poly", tag="big", align_bytes=64)
+        def root(first, count):
+            nc.scalar.activation(out=tiles(first, count), in_=tiles(first, count), func=ACT.Sqrt, scale=5.0)
+
+        def polynomial(first, count, units):
+            several = place([P, count, N_POINTS], F32, "poly_%d" % first, units)
+            for s in range(count):
+                poly[first + s] = several[:, s, :]
             nc.scalar.activation(
-                out=poly[i][:], in_=dist[i][:], func=ACT.Square,
+                out=several[:], in_=tiles(first, count), func=ACT.Square,
                 scale=poly_scale[:, 0:1], bias=poly_bias[:, 0:1],
             )
 
-        def horner(i):
-            poly[i] = big.tile([P, N_POINTS], F32, name="poly", tag="big", align_bytes=64)
+        def horner(i, units):
+            poly[i] = place([P, 1, N_POINTS], F32, "poly_%d" % i, units)[:, 0, :]
+            x = tiles(i, 1)[:, 0, :]
             nc.vector.tensor_scalar(
-                out=poly[i][:], in0=dist[i][:], scalar1=c2_third[:, 0:1], scalar2=c2[:, 0:1],
-                op0=ALU.mult, op1=ALU.add,
+                out=poly[i], in0=x, scalar1=c2_third[:, 0:1], scalar2=c2[:, 0:1], op0=ALU.mult, op1=ALU.add
             )
-            nc.vector.tensor_tensor(out=poly[i][:], in0=poly[i][:], in1=dist[i][:], op=ALU.mult)
+            nc.vector.tensor_tensor(out=poly[i], in0=poly[i], in1=x, op=ALU.mult)
 
-        def finish(i):
-            nc.scalar.activation(out=dist[i][:], in_=dist[i][:], func=ACT.Exp, scale=-1.0)
-            rest = c2 if i in HORNER else poly_rest
+        def decay(first, count):
+            nc.scalar.activation(out=tiles(first, count), in_=tiles(first, count), func=ACT.Exp, scale=-1.0)
+
+        def finish(i, rest):
             nc.vector.scalar_tensor_tensor(
-                out=poly[i][:], in0=poly[i][:], scalar=rest[:, 0:1], in1=dist[i][:],
+                out=poly[i], in0=poly[i], scalar=rest[:, 0:1], in1=tiles(i, 1)[:, 0, :],
                 op0=ALU.add, op1=ALU.mult,
             )
-            nc.sync.dma_start(out=out[i * BLOCK : (i + 1) * BLOCK, :], in_=poly[i][:])
+            nc.sync.dma_start(out=out[i * BLOCK : (i + 1) * BLOCK, :], in_=poly[i])
 
-        for k in range(N_BANKS):
-            flip("x2", k)
-            flip("x1", k)
-            divide("x2", k)
-            square("x2", k)
-            if k >= 2 and k % 2 == 0:
-                quantise("x2", k // 2 - 1)
-            divide("x1", k)
-            square("x1", k)
-            if k >= 2 and k % 2 == 0:
-                quantise("x1", k // 2 - 1)
-            if k >= 1:
-                sum_rows(k - 1)
-        sum_rows(N_BANKS - 1)
-        quantise("x2", N_GROUPS - 1)
-        quantise("x1", N_GROUPS - 1)
-        sum_column(0)
-        sum_column(1)
+        for g in range(N_GROUPS):
+            divide_rows(g)
+        order = []
+        for k in range(N_BANKS + LAG):
+            if k < N_BANKS:
+                order.append(("x2", k))
+            if k >= LAG:
+                order.append(("x1", k - LAG))
+        for n in range(AHEAD):
+            flip(*order[n])
+        for n in range(len(order) + 3):
+            if n + AHEAD < len(order):
+                flip(*order[n + AHEAD])
+            if n < len(order):
+                divide(*order[n])
+                if order[n][0] == "x2":
+                    square(*order[n])
+            if 1 <= n <= len(order) and order[n - 1][1] % 2 == 1:
+                quantise(order[n - 1][0], order[n - 1][1] // 2)
+                if order[n - 1][0] == "x2":
+                    sum_rows(order[n - 1][1] // 2)
+            if 3 <= n and order[n - 3][0] == "x2" and order[n - 3][1] % 2 == 1:
+                keep_rows(order[n - 3][1] // 2)
+            if n >= 5 and (n - 5) % 3 == 0 and (n - 5) // 3 < N_GROUPS:
+                sum_columns((n - 5) // 3)
 
         for i in range(N_TILES):
             distances(i)
-            if i + 2 < N_TILES:
-                sum_column(i + 2)
-            root(i)
-            if i in EARLY:
-                polynomial(i)
+            if i % 2 == 1:
+                root(i - 1, 2)
+            if i == 3:
+                polynomial(0, QUAD, 16)
+            if i == 7:
+                polynomial(QUAD, QUAD, 20)
 
-        for i in range(N_TILES):
-            for h in HORNER_AT.get(i, ()):
-                horner(h)
-            if i not in EARLY and i not in HORNER:
-                polynomial(i)
-            finish(i)
+        for s in range(QUAD):
+            horner(12 + s, 24 + s)
+        decay(0, QUAD)
+        for i in range(0, 4):
+            finish(i, poly_rest)
+        decay(4, QUAD)
+        for i in range(4, 8):
+            finish(i, poly_rest)
+        decay(12, QUAD)
+        for i in range(12, 16):
+            finish(i, c2)
+        polynomial(8, QUAD, 16)
+        decay(8, 2)
+        finish(8, poly_rest)
+        finish(9, poly_rest)
+        decay(10, 1)
+        finish(10, poly_rest)
+        decay(11, 1)
+        finish(11, poly_rest)

@@ -114,7 +114,6 @@ def tile_matern52_kernel(tc, X1, X2, c, l, out):
             grouped["x2", g] = both[:, 0, :, :]
             grouped["x1", g] = both[:, 1, :, :]
             squared["x2", g] = place([P, PACK, GROUP_POINTS], F32, "squared_x2_%d" % g, 20 + g)
-            scaled[g] = place([P, QUAD, D], F32, "scaled_%d" % g, 12 + g)
 
         def flip(name, k):
             h, b = divmod(2 * k, LOAD_POINTS // BLOCK)
@@ -172,6 +171,7 @@ def tile_matern52_kernel(tc, X1, X2, c, l, out):
 
         def divide_rows(g):
             h, q = divmod(g, 2)
+            scaled[g] = place([P, QUAD, D], F32, "scaled_%d" % g, 12 if g == 0 else 15 + g)
             nc.gpsimd.tensor_tensor(
                 out=scaled[g][:], in0=raw["x1", h][:, QUAD * q : QUAD * (q + 1), :],
                 in1=inv_l_row[:].unsqueeze(1).to_broadcast([P, QUAD, D]), op=ALU.mult,
@@ -245,8 +245,7 @@ def tile_matern52_kernel(tc, X1, X2, c, l, out):
             )
             nc.sync.dma_start(out=out[i * BLOCK : (i + 1) * BLOCK, :], in_=poly[i])
 
-        for g in range(N_GROUPS):
-            divide_rows(g)
+        divide_rows(0)
         order = []
         for k in range(N_BANKS + LAG):
             if k < N_BANKS:
@@ -263,16 +262,27 @@ def tile_matern52_kernel(tc, X1, X2, c, l, out):
                 if order[n][0] == "x2":
                     square(*order[n])
             if 1 <= n <= len(order) and order[n - 1][1] % 2 == 1:
-                quantise(order[n - 1][0], order[n - 1][1] // 2)
-                if order[n - 1][0] == "x2":
-                    sum_rows(order[n - 1][1] // 2)
+                name, g = order[n - 1][0], order[n - 1][1] // 2
+                if name == "x2":
+                    sum_rows(g)
+                    if g == 1:
+                        quantise("x2", 0)
+                    if g >= 1:
+                        quantise("x2", g)
+                elif g + 1 < N_GROUPS:
+                    quantise("x1", g)
+                    divide_rows(g + 1)
             if 3 <= n and order[n - 3][0] == "x2" and order[n - 3][1] % 2 == 1:
                 keep_rows(order[n - 3][1] // 2)
-            if n >= 5 and (n - 5) % 3 == 0 and (n - 5) // 3 < N_GROUPS:
-                sum_columns((n - 5) // 3)
+            if n == 5:
+                sum_columns(0)
+        for g in range(1, N_GROUPS):
+            sum_columns(g)
 
         for i in range(N_TILES):
             distances(i)
+            if i == 0:
+                quantise("x1", N_GROUPS - 1)
             if i % 2 == 1:
                 root(i - 1, 2)
             if i == 3:

@@ -26,7 +26,7 @@ N_GROUPS = N_POINTS // GROUP_POINTS
 N_LOADS = N_POINTS // LOAD_POINTS
 QUAD = 4
 LAG = 2
-AHEAD = 4
+AHEAD = 3
 UNIT = 4 * N_POINTS
 
 FLOPS = 2 * N_POINTS * N_POINTS * D
@@ -187,6 +187,13 @@ def tile_matern52_kernel(tc, X1, X2, c, l, out):
         dist = {}
         poly = {}
 
+        def clamp(i):
+            q, s = divmod(i, QUAD)
+            nc.vector.tensor_scalar(
+                out=dist[q][:, s, :], in0=dist[q][:, s, :], scalar1=sq1[:, i : i + 1], scalar2=0.0,
+                op0=ALU.add, op1=ALU.max,
+            )
+
         def distances(i):
             q, s = divmod(i, QUAD)
             if s == 0:
@@ -206,10 +213,8 @@ def tile_matern52_kernel(tc, X1, X2, c, l, out):
                     out=dist[q][:, s, cols], in0=cross[:], scalar=-2.0, in1=sq2_rows[:, cols],
                     op0=ALU.mult, op1=ALU.add,
                 )
-            nc.vector.tensor_scalar(
-                out=dist[q][:, s, :], in0=dist[q][:, s, :], scalar1=sq1[:, i : i + 1], scalar2=0.0,
-                op0=ALU.add, op1=ALU.max,
-            )
+                if j == 0 and i >= 1:
+                    clamp(i - 1)
 
         def tiles(first, count):
             q, s = divmod(first, QUAD)
@@ -227,13 +232,15 @@ def tile_matern52_kernel(tc, X1, X2, c, l, out):
                 scale=poly_scale[:, 0:1], bias=poly_bias[:, 0:1],
             )
 
-        def horner(i, units):
+        def horner_first(i, units):
             poly[i] = place([P, 1, N_POINTS], F32, "poly_%d" % i, units)[:, 0, :]
-            x = tiles(i, 1)[:, 0, :]
             nc.vector.tensor_scalar(
-                out=poly[i], in0=x, scalar1=c2_third[:, 0:1], scalar2=c2[:, 0:1], op0=ALU.mult, op1=ALU.add
+                out=poly[i], in0=tiles(i, 1)[:, 0, :], scalar1=c2_third[:, 0:1], scalar2=c2[:, 0:1],
+                op0=ALU.mult, op1=ALU.add,
             )
-            nc.vector.tensor_tensor(out=poly[i], in0=poly[i], in1=x, op=ALU.mult)
+
+        def horner_second(i):
+            nc.vector.tensor_tensor(out=poly[i], in0=poly[i], in1=tiles(i, 1)[:, 0, :], op=ALU.mult)
 
         def decay(first, count):
             nc.scalar.activation(out=tiles(first, count), in_=tiles(first, count), func=ACT.Exp, scale=-1.0)
@@ -279,19 +286,25 @@ def tile_matern52_kernel(tc, X1, X2, c, l, out):
         for g in range(1, N_GROUPS):
             sum_columns(g)
 
-        for i in range(N_TILES):
-            distances(i)
+        for i in range(N_TILES + 1):
+            if i < N_TILES:
+                distances(i)
+            else:
+                clamp(i - 1)
+                horner_first(12, 24)
             if i == 0:
                 quantise("x1", N_GROUPS - 1)
-            if i % 2 == 1:
-                root(i - 1, 2)
-            if i == 3:
+            if i >= 2 and i % 2 == 0:
+                root(i - 2, 2)
+            if i == 4:
                 polynomial(0, QUAD, 16)
-            if i == 7:
+            if i == 8:
                 polynomial(QUAD, QUAD, 20)
 
-        for s in range(QUAD):
-            horner(12 + s, 24 + s)
+        for s in range(1, QUAD):
+            horner_first(12 + s, 24 + s)
+            horner_second(12 + s - 1)
+        horner_second(15)
         decay(0, QUAD)
         for i in range(0, 4):
             finish(i, poly_rest)
@@ -301,10 +314,11 @@ def tile_matern52_kernel(tc, X1, X2, c, l, out):
         decay(12, QUAD)
         for i in range(12, 16):
             finish(i, c2)
-        polynomial(8, QUAD, 16)
+        polynomial(8, 2, 16)
         decay(8, 2)
         finish(8, poly_rest)
         finish(9, poly_rest)
+        polynomial(10, 2, 18)
         decay(10, 1)
         finish(10, poly_rest)
         decay(11, 1)

@@ -52,11 +52,11 @@ def tile_matern52_kernel(tc, X1, X2, c, l, out):
         for h in range(N_LOADS):
             for s, (name, points) in enumerate((("x2", X2), ("x1", X1))):
                 raw[name, h] = place([P, LOAD_POINTS // BLOCK, D], BF16, "raw_%s_%d" % (name, h), 8 + 2 * h + s)
-                for q in range(2):
-                    first = h * LOAD_POINTS + q * GROUP_POINTS
+                for q in range(4):
+                    first = h * LOAD_POINTS + q * BANK_POINTS
                     nc.sync.dma_start(
-                        out=raw[name, h][:, 4 * q : 4 * q + 4, :],
-                        in_=points[first : first + GROUP_POINTS, :].rearrange("(b p) d -> p b d", p=P),
+                        out=raw[name, h][:, 2 * q : 2 * q + 2, :],
+                        in_=points[first : first + BANK_POINTS, :].rearrange("(b p) d -> p b d", p=P),
                     )
 
         ident = keep.tile([P, P], F32)
@@ -70,27 +70,29 @@ def tile_matern52_kernel(tc, X1, X2, c, l, out):
         inv_l2 = keep.tile([P, PACK], F32)
         nc.vector.tensor_tensor(out=inv_l2[:], in0=inv_l[:], in1=inv_l[:], op=ALU.mult)
         c_f32 = keep.tile([P, 1], F32)
-        nc.vector.tensor_copy(out=c_f32[:], in_=c_all[:])
         poly_scale = keep.tile([P, 1], F32)
-        nc.vector.tensor_scalar(
-            out=poly_scale[:], in0=c_f32[:], scalar1=1.0 / math.sqrt(3.0), scalar2=None, op0=ALU.mult
-        )
         poly_bias = keep.tile([P, 1], F32)
-        nc.vector.tensor_scalar(
-            out=poly_bias[:], in0=c_f32[:], scalar1=1.5 / math.sqrt(3.0), scalar2=None, op0=ALU.mult
-        )
         poly_rest = keep.tile([P, 1], F32)
-        nc.vector.tensor_scalar(
-            out=poly_rest[:], in0=c_f32[:], scalar1=c_f32[:, 0:1], scalar2=0.25,
-            op0=ALU.mult, op1=ALU.mult,
-        )
         c2 = keep.tile([P, 1], F32)
-        nc.vector.tensor_tensor(out=c2[:], in0=c_f32[:], in1=c_f32[:], op=ALU.mult)
         c2_third = keep.tile([P, 1], F32)
-        nc.vector.tensor_scalar(
-            out=c2_third[:], in0=c_f32[:], scalar1=c_f32[:, 0:1], scalar2=1.0 / 3.0,
-            op0=ALU.mult, op1=ALU.mult,
-        )
+
+        def constants():
+            nc.vector.tensor_copy(out=c_f32[:], in_=c_all[:])
+            nc.vector.tensor_scalar(
+                out=poly_scale[:], in0=c_f32[:], scalar1=1.0 / math.sqrt(3.0), scalar2=None, op0=ALU.mult
+            )
+            nc.vector.tensor_scalar(
+                out=poly_bias[:], in0=c_f32[:], scalar1=1.5 / math.sqrt(3.0), scalar2=None, op0=ALU.mult
+            )
+            nc.vector.tensor_scalar(
+                out=poly_rest[:], in0=c_f32[:], scalar1=c_f32[:, 0:1], scalar2=0.25,
+                op0=ALU.mult, op1=ALU.mult,
+            )
+            nc.vector.tensor_tensor(out=c2[:], in0=c_f32[:], in1=c_f32[:], op=ALU.mult)
+            nc.vector.tensor_scalar(
+                out=c2_third[:], in0=c_f32[:], scalar1=c_f32[:, 0:1], scalar2=1.0 / 3.0,
+                op0=ALU.mult, op1=ALU.mult,
+            )
 
         codes = {"x1": place([P, N_POINTS], U32, "codes_x1", 25), "x2": place([P, N_POINTS], U32, "codes_x2", 26)}
         sq2_rows = place([P, N_POINTS], F32, "sq2_rows", 27)
@@ -189,6 +191,11 @@ def tile_matern52_kernel(tc, X1, X2, c, l, out):
 
         def clamp(i):
             q, s = divmod(i, QUAD)
+            if i == 0:
+                nc.scalar.activation(
+                    out=dist[q][:, s, :], in_=dist[q][:, s, :], func=ACT.Relu, bias=sq1[:, i : i + 1]
+                )
+                return
             nc.vector.tensor_scalar(
                 out=dist[q][:, s, :], in0=dist[q][:, s, :], scalar1=sq1[:, i : i + 1], scalar2=0.0,
                 op0=ALU.add, op1=ALU.max,
@@ -279,6 +286,8 @@ def tile_matern52_kernel(tc, X1, X2, c, l, out):
                 elif g + 1 < N_GROUPS:
                     quantise("x1", g)
                     divide_rows(g + 1)
+            if n == 4:
+                constants()
             if 3 <= n and order[n - 3][0] == "x2" and order[n - 3][1] % 2 == 1:
                 keep_rows(order[n - 3][1] // 2)
             if n == 5:

import math
from contextlib import ExitStack

from concourse import mybir
from concourse.masks import make_identity

F32 = mybir.dt.float32
BF16 = mybir.dt.bfloat16
U32 = mybir.dt.uint32
U8 = mybir.dt.uint8
FP8X4 = mybir.dt.float8_e4m3fn_x4
ALU = mybir.AluOpType
ACT = mybir.ActivationFunctionType

P = 128
PACK = 4
D = P * PACK
N_POINTS = 2048
BLOCK = P
BANK_POINTS = 2 * BLOCK
GROUP_POINTS = 4 * BLOCK
LOAD_POINTS = 8 * BLOCK
N_TILES = N_POINTS // BLOCK
N_BANKS = N_POINTS // BANK_POINTS
N_GROUPS = N_POINTS // GROUP_POINTS
N_LOADS = N_POINTS // LOAD_POINTS
QUAD = 4
LAG = 2
AHEAD = 3
UNIT = 4 * N_POINTS

FLOPS = 2 * N_POINTS * N_POINTS * D


def tile_matern52_kernel(tc, X1, X2, c, l, out):
    nc = tc.nc
    with ExitStack() as ctx:
        keep = ctx.enter_context(tc.tile_pool(name="keep", bufs=1))
        big = ctx.enter_context(tc.tile_pool(name="big", bufs=1))
        psum = ctx.enter_context(tc.psum_pool(name="psum", bufs=7))
        psum_s = ctx.enter_context(tc.psum_pool(name="psum_s", bufs=1))
        ctx.enter_context(tc.manual_schedule())

        def place(shape, dtype, name, units):
            return big.tile(shape, dtype, name=name, offset=int(units * UNIT), align_bytes=64)

        l_cols = keep.tile([P, PACK], BF16)
        nc.sync.dma_start(out=l_cols[:], in_=l.rearrange("(p t) -> p t", t=PACK))
        c_all = keep.tile([P, 1], BF16)
        nc.scalar.dma_start(out=c_all[:], in_=c.partition_broadcast(P))
        raw = {}
        for h in range(N_LOADS):
            for s, (name, points) in enumerate((("x2", X2), ("x1", X1))):
                raw[name, h] = place([P, LOAD_POINTS // BLOCK, D], BF16, "raw_%s_%d" % (name, h), 8 + 2 * h + s)
                for q in range(4):
                    first = h * LOAD_POINTS + q * BANK_POINTS
                    nc.sync.dma_start(
                        out=raw[name, h][:, 2 * q : 2 * q + 2, :],
                        in_=points[first : first + BANK_POINTS, :].rearrange("(b p) d -> p b d", p=P),
                    )

        ident = keep.tile([P, P], F32)
        make_identity(nc, ident[:])
        one = keep.tile([P, 1], F32)
        nc.vector.memset(one[:], 1.0)
        warm = keep.tile([P, 1], F32)
        nc.scalar.activation(out=warm[:], in_=one[:], func=ACT.Sqrt)
        inv_l = keep.tile([P, PACK], F32)
        nc.vector.reciprocal(out=inv_l[:], in_=l_cols[:])
        inv_l2 = keep.tile([P, PACK], F32)
        nc.vector.tensor_tensor(out=inv_l2[:], in0=inv_l[:], in1=inv_l[:], op=ALU.mult)
        c_f32 = keep.tile([P, 1], F32)
        poly_scale = keep.tile([P, 1], F32)
        poly_bias = keep.tile([P, 1], F32)
        poly_rest = keep.tile([P, 1], F32)
        c2 = keep.tile([P, 1], F32)
        c2_third = keep.tile([P, 1], F32)

        def constants():
            nc.vector.tensor_copy(out=c_f32[:], in_=c_all[:])
            nc.vector.tensor_scalar(
                out=poly_scale[:], in0=c_f32[:], scalar1=1.0 / math.sqrt(3.0), scalar2=None, op0=ALU.mult
            )
            nc.vector.tensor_scalar(
                out=poly_bias[:], in0=c_f32[:], scalar1=1.5 / math.sqrt(3.0), scalar2=None, op0=ALU.mult
            )
            nc.vector.tensor_scalar(
                out=poly_rest[:], in0=c_f32[:], scalar1=c_f32[:, 0:1], scalar2=0.25,
                op0=ALU.mult, op1=ALU.mult,
            )
            nc.vector.tensor_tensor(out=c2[:], in0=c_f32[:], in1=c_f32[:], op=ALU.mult)
            nc.vector.tensor_scalar(
                out=c2_third[:], in0=c_f32[:], scalar1=c_f32[:, 0:1], scalar2=1.0 / 3.0,
                op0=ALU.mult, op1=ALU.mult,
            )

        codes = {"x1": place([P, N_POINTS], U32, "codes_x1", 25), "x2": place([P, N_POINTS], U32, "codes_x2", 26)}
        sq2_rows = place([P, N_POINTS], F32, "sq2_rows", 27)
        scales = {"x1": place([P, N_POINTS], U8, "scales_x1", 28), "x2": place([P, N_POINTS], U8, "scales_x2", 28.25)}
        sq1 = keep.tile([P, N_TILES], F32)

        turned = psum_s.tile([P, PACK, P], F32, name="total")
        for t in range(PACK):
            nc.tensor.transpose(turned[:, t, :], inv_l[:, t : t + 1].to_broadcast([P, P]), ident[:])
        inv_l_row = keep.tile([P, D], F32)
        nc.scalar.copy(
            out=inv_l_row[:].rearrange("p (j t) -> p j t", t=PACK), in_=turned[:].rearrange("p t j -> p j t")
        )

        scaled = {}
        flipped = {}
        grouped = {}
        squared = {}
        for g in range(N_GROUPS):
            both = place([P, 2, GROUP_POINTS, PACK], BF16, "grouped_%d" % g, 16 + g)
            grouped["x2", g] = both[:, 0, :, :]
            grouped["x1", g] = both[:, 1, :, :]
            squared["x2", g] = place([P, PACK, GROUP_POINTS], F32, "squared_x2_%d" % g, 20 + g)

        def flip(name, k):
            h, b = divmod(2 * k, LOAD_POINTS // BLOCK)
            words = raw[name, h][:].bitcast(F32)
            flipped[name, k] = psum.tile([P, 2, BANK_POINTS], F32, name="flipped", tag="bank")
            for s in range(2):
                for u in range(2):
                    nc.tensor.transpose(
                        flipped[name, k][:, u, s * BLOCK : (s + 1) * BLOCK],
                        words[:, b + s, u : D // 2 : 2],
                        ident[:],
                    )

        def divide(name, k):
            g, half = divmod(k, 2)
            nc.vector.tensor_tensor(
                out=grouped[name, g][:, half * BANK_POINTS : (half + 1) * BANK_POINTS, :].rearrange(
                    "p r (u e) -> p r u e", e=2
                ),
                in0=flipped[name, k][:].bitcast(BF16).rearrange("p u (r e) -> p r u e", e=2),
                in1=inv_l[:].rearrange("p (u e) -> p u e", e=2).unsqueeze(1).to_broadcast([P, BANK_POINTS, 2, 2]),
                op=ALU.mult,
            )

        def square(name, k):
            g, half = divmod(k, 2)
            nc.scalar.activation(
                out=squared[name, g][:, :, half * BANK_POINTS : (half + 1) * BANK_POINTS].rearrange(
                    "p (u e) r -> p u e r", e=2
                ),
                in_=flipped[name, k][:].bitcast(BF16).rearrange("p u (r e) -> p u e r", e=2),
                func=ACT.Square,
            )

        def quantise(name, g):
            cols = slice(g * GROUP_POINTS, (g + 1) * GROUP_POINTS)
            nc.vector.quantize_mx(
                out=codes[name][:, cols].bitcast(FP8X4),
                scales=scales[name][:, cols],
                in_=grouped[name, g].rearrange("p r t -> p (r t)"),
            )

        totals = {}

        def sum_rows(g):
            totals[g] = psum_s.tile([P, GROUP_POINTS], F32, name="total")
            for t in range(PACK):
                nc.tensor.matmul(
                    out=totals[g][:], lhsT=inv_l2[:, t : t + 1].to_broadcast([P, P]), rhs=squared["x2", g][:, t, :],
                    start=(t == 0), stop=(t == PACK - 1),
                )

        def keep_rows(g):
            nc.vector.tensor_copy(out=sq2_rows[:, g * GROUP_POINTS : (g + 1) * GROUP_POINTS], in_=totals[g][:])

        def divide_rows(g):
            h, q = divmod(g, 2)
            scaled[g] = place([P, QUAD, D], F32, "scaled_%d" % g, 12 if g == 0 else 15 + g)
            nc.gpsimd.tensor_tensor(
                out=scaled[g][:], in0=raw["x1", h][:, QUAD * q : QUAD * (q + 1), :],
                in1=inv_l_row[:].unsqueeze(1).to_broadcast([P, QUAD, D]), op=ALU.mult,
            )

        def sum_columns(g):
            for b in range(QUAD):
                nc.scalar.activation(
                    out=scaled[g][:, b, :], in_=scaled[g][:, b, :], func=ACT.Square,
                    accum_out=sq1[:, QUAD * g + b : QUAD * g + b + 1],
                )

        dist = {}
        poly = {}

        def clamp(i):
            q, s = divmod(i, QUAD)
            if i == 0:
                nc.scalar.activation(
                    out=dist[q][:, s, :], in_=dist[q][:, s, :], func=ACT.Relu, bias=sq1[:, i : i + 1]
                )
                return
            nc.vector.tensor_scalar(
                out=dist[q][:, s, :], in0=dist[q][:, s, :], scalar1=sq1[:, i : i + 1], scalar2=0.0,
                op0=ALU.add, op1=ALU.max,
            )

        def distances(i):
            q, s = divmod(i, QUAD)
            if s == 0:
                dist[q] = place([P, QUAD, N_POINTS], F32, "dist_%d" % q, QUAD * q)
            for j in range(N_GROUPS):
                cols = slice(j * GROUP_POINTS, (j + 1) * GROUP_POINTS)
                cross = psum.tile([P, GROUP_POINTS], F32, name="cross", tag="bank")
                nc.tensor.matmul_mx(
                    out=cross[:],
                    lhsT=codes["x1"][:, i * BLOCK : (i + 1) * BLOCK].bitcast(FP8X4),
                    lhsT_scale=scales["x1"][:, i * BLOCK : (i + 1) * BLOCK],
                    rhs=codes["x2"][:, cols].bitcast(FP8X4),
                    rhs_scale=scales["x2"][:, cols],
                    start=True, stop=True,
                )
                nc.vector.scalar_tensor_tensor(
                    out=dist[q][:, s, cols], in0=cross[:], scalar=-2.0, in1=sq2_rows[:, cols],
                    op0=ALU.mult, op1=ALU.add,
                )
                if j == 0 and i >= 1:
                    clamp(i - 1)

        def tiles(first, count):
            q, s = divmod(first, QUAD)
            return dist[q][:, s : s + count, :]

        def root(first, count):
            nc.scalar.activation(out=tiles(first, count), in_=tiles(first, count), func=ACT.Sqrt, scale=5.0)

        def polynomial(first, count, units):
            several = place([P, count, N_POINTS], F32, "poly_%d" % first, units)
            for s in range(count):
                poly[first + s] = several[:, s, :]
            nc.scalar.activation(
                out=several[:], in_=tiles(first, count), func=ACT.Square,
                scale=poly_scale[:, 0:1], bias=poly_bias[:, 0:1],
            )

        def horner_first(i, units):
            poly[i] = place([P, 1, N_POINTS], F32, "poly_%d" % i, units)[:, 0, :]
            nc.vector.tensor_scalar(
                out=poly[i], in0=tiles(i, 1)[:, 0, :], scalar1=c2_third[:, 0:1], scalar2=c2[:, 0:1],
                op0=ALU.mult, op1=ALU.add,
            )

        def horner_second(i):
            nc.vector.tensor_tensor(out=poly[i], in0=poly[i], in1=tiles(i, 1)[:, 0, :], op=ALU.mult)

        def decay(first, count):
            nc.scalar.activation(out=tiles(first, count), in_=tiles(first, count), func=ACT.Exp, scale=-1.0)

        def finish(i, rest):
            nc.vector.scalar_tensor_tensor(
                out=poly[i], in0=poly[i], scalar=rest[:, 0:1], in1=tiles(i, 1)[:, 0, :],
                op0=ALU.add, op1=ALU.mult,
            )
            nc.sync.dma_start(out=out[i * BLOCK : (i + 1) * BLOCK, :], in_=poly[i])

        divide_rows(0)
        order = []
        for k in range(N_BANKS + LAG):
            if k < N_BANKS:
                order.append(("x2", k))
            if k >= LAG:
                order.append(("x1", k - LAG))
        for n in range(AHEAD):
            flip(*order[n])
        for n in range(len(order) + 3):
            if n + AHEAD < len(order):
                flip(*order[n + AHEAD])
            if n < len(order):
                divide(*order[n])
                if order[n][0] == "x2":
                    square(*order[n])
            if 1 <= n <= len(order) and order[n - 1][1] % 2 == 1:
                name, g = order[n - 1][0], order[n - 1][1] // 2
                if name == "x2":
                    sum_rows(g)
                    if g == 1:
                        quantise("x2", 0)
                    if g >= 1:
                        quantise("x2", g)
                elif g + 1 < N_GROUPS:
                    quantise("x1", g)
                    divide_rows(g + 1)
            if n == 4:
                constants()
            if 3 <= n and order[n - 3][0] == "x2" and order[n - 3][1] % 2 == 1:
                keep_rows(order[n - 3][1] // 2)
            if n == 5:
                sum_columns(0)
        for g in range(1, N_GROUPS):
            sum_columns(g)

        for i in range(N_TILES + 1):
            if i < N_TILES:
                distances(i)
            else:
                clamp(i - 1)
                horner_first(12, 24)
            if i == 0:
                quantise("x1", N_GROUPS - 1)
            if i >= 2 and i % 2 == 0:
                root(i - 2, 2)
            if i == 4:
                polynomial(0, QUAD, 16)
            if i == 8:
                polynomial(QUAD, QUAD, 20)

        for s in range(1, QUAD):
            horner_first(12 + s, 24 + s)
            horner_second(12 + s - 1)
        horner_second(15)
        decay(0, QUAD)
        for i in range(0, 4):
            finish(i, poly_rest)
        decay(4, QUAD)
        for i in range(4, 8):
            finish(i, poly_rest)
        decay(12, QUAD)
        for i in range(12, 16):
            finish(i, c2)
        polynomial(8, 2, 16)
        decay(8, 2)
        finish(8, poly_rest)
        finish(9, poly_rest)
        polynomial(10, 2, 18)
        decay(10, 1)
        finish(10, poly_rest)
        decay(11, 1)
        finish(11, poly_rest)
